import numpy as np
import ml_dtypes


def mxq(x, axis, fmt="e4m3"):
    dtype, down = {"e4m3": (ml_dtypes.float8_e4m3fn, 7), "e5m2": (ml_dtypes.float8_e5m2, 14)}[fmt]
    v = np.moveaxis(np.asarray(x, np.float32).astype(ml_dtypes.bfloat16).astype(np.float64), axis, -1)
    blocks = v.reshape(v.shape[:-1] + (-1, 32))
    amax = np.abs(blocks).max(-1, keepdims=True)
    byte = np.maximum(np.where(amax > 0, np.frexp(amax)[1] - 1 + 127, 0) - down, 1)
    scale = np.exp2(byte - 127.0)
    codes = (blocks / scale).astype(np.float32).astype(dtype).astype(np.float64)
    return np.moveaxis((codes * scale).reshape(v.shape), -1, axis)


WIDE = False


def mx_kscale(k):
    if not WIDE:
        return np.ones(k)
    levels = np.array([10, -10, 5, -5, 0])
    a = np.random.permutation(np.resize(levels, k // 512 * 4)).reshape(k // 512, 4)
    idx = np.arange(k)
    return np.exp2(a[idx // 512, idx % 128 // 32])


BF16 = ml_dtypes.bfloat16


def bf(x):
    return np.asarray(x, np.float32).astype(BF16)


def f64(x):
    return np.asarray(x).astype(np.float64)


N, K, C, CE, M, F = 128, 32, 512, 1536, 512, 2048
SCALE = 30.0
EPS = 1e-5


def erf(x):
    a = np.minimum(np.abs(x), 6.0)
    a2 = 2.0 * a * a
    t = a
    s = a
    for n in range(1, 110):
        t = t * a2 / (2 * n + 1)
        s = s + t
    return np.sign(x) * np.minimum(s * np.exp(-a * a) * 2.0 / np.sqrt(np.pi), 1.0)


def gelu(v):
    return 0.5 * v * (1.0 + erf(v / np.sqrt(2.0)))


def layernorm(x, w, b):
    mu = x.mean(-1, keepdims=True)
    var = ((x - mu) ** 2).mean(-1, keepdims=True)
    return (x - mu) / np.sqrt(var + EPS) * w + b


def setup_inputs():
    s = mx_kscale(M)
    return {
        "m2": bf(gelu(np.random.standard_normal((N, K, M))) * s),
        "W3": bf(np.random.standard_normal((C, M)) * 3.0 / np.sqrt(M) / s),
        "b3": bf(np.random.standard_normal(C) * 0.1),
        "attention_mask": bf(np.random.random((N, K)) < 0.75),
        "node_features": bf(np.random.standard_normal((N, C))),
        "ln1_w": bf(1.0 + np.random.standard_normal(C) * 0.1),
        "ln1_b": bf(np.random.standard_normal(C) * 0.1),
    }


def reference(m2, W3, b3, attention_mask, node_features, ln1_w, ln1_b):
    m = (mxq(f64(m2), 2, "e4m3") @ mxq(f64(W3).T, 0, "e4m3")) + f64(b3)
    m = f64(attention_mask)[..., None] * m
    agg = m.sum(-2) / SCALE
    return layernorm(f64(node_features) + agg, f64(ln1_w), f64(ln1_b))

@@ -1,0 +1,176 @@
+from contextlib import ExitStack
+
+import concourse.mybir as mybir
+from concourse.masks import make_identity
+
+F32 = mybir.dt.float32
+BF16 = mybir.dt.bfloat16
+U32 = mybir.dt.uint32
+U8 = mybir.dt.uint8
+FP8X4 = mybir.dt.float8_e4m3fn_x4
+ALU = mybir.AluOpType
+ACT = mybir.ActivationFunctionType
+
+P = 128
+NEIGHBOURS = 32
+K = 512
+CHANNELS = 512
+PACK = 4
+WORDS = K // 2
+HALVES = WORDS // P
+SLABS = 4
+CHUNKS = NEIGHBOURS // SLABS
+BANK_SLABS = 2
+SCALE = 30.0
+EPS = 1e-5
+
+FLOPS = 2 * P * NEIGHBOURS * K * CHANNELS
+
+
+def tile_decoderlayer_pb_kernel(
+    tc, m2, W3, b3, attention_mask, node_features, ln1_w, ln1_b, out
+):
+    nc = tc.nc
+    with ExitStack() as ctx:
+        ctx.enter_context(tc.manual_schedule())
+        keep = ctx.enter_context(tc.tile_pool(name="keep", bufs=1))
+        grouped_pool = ctx.enter_context(tc.tile_pool(name="grouped", bufs=3))
+        mx_pool = ctx.enter_context(tc.tile_pool(name="mx", bufs=3))
+        bank_pool = ctx.enter_context(tc.psum_pool(name="banks", bufs=6))
+        acc_pool = ctx.enter_context(tc.psum_pool(name="acc", bufs=1))
+
+        mask_bf = keep.tile([P, NEIGHBOURS], BF16)
+        nc.sync.dma_start(out=mask_bf[:], in_=attention_mask)
+        w3_rows = keep.tile([P, SLABS * K], BF16)
+        nc.sync.dma_start(
+            out=w3_rows[:].rearrange("p (r k) -> p r k", r=SLABS),
+            in_=W3.rearrange("(r p) k -> p r k", p=P),
+        )
+        m2_rows = []
+        for c in range(CHUNKS):
+            rows = keep.tile([P, SLABS * K], BF16, name="m2_rows%d" % c)
+            nc.sync.dma_start(
+                out=rows[:].rearrange("p (s k) -> p s k", s=SLABS),
+                in_=m2[:, c * SLABS : (c + 1) * SLABS, :],
+            )
+            m2_rows.append(rows)
+        nodes_bf = keep.tile([P, CHANNELS], BF16)
+        nc.sync.dma_start(out=nodes_bf[:], in_=node_features)
+        b3_all = keep.tile([P, CHANNELS], BF16)
+        nc.sync.dma_start(out=b3_all[:], in_=b3.partition_broadcast(P))
+        gain_all = keep.tile([P, CHANNELS], BF16)
+        nc.sync.dma_start(out=gain_all[:], in_=ln1_w.partition_broadcast(P))
+        shift_all = keep.tile([P, CHANNELS], BF16)
+        nc.sync.dma_start(out=shift_all[:], in_=ln1_b.partition_broadcast(P))
+
+        identity = keep.tile([P, P], F32)
+        make_identity(nc, identity[:])
+        eps = keep.tile([P, 1], F32)
+        nc.vector.memset(eps[:], EPS)
+        table_warm = keep.tile([P, 1], F32)
+        nc.scalar.sqrt(out=table_warm[:], in_=eps[:])
+        mask = keep.tile([P, NEIGHBOURS], F32)
+        nc.vector.tensor_copy(out=mask[:], in_=mask_bf[:])
+
+        def transpose_chunk(rows):
+            words = rows[:].bitcast(F32)
+            banks = []
+            for b in range(SLABS // BANK_SLABS):
+                bank = bank_pool.tile([P, BANK_SLABS, HALVES, P], F32)
+                for s in range(BANK_SLABS):
+                    for u in range(HALVES):
+                        first = (b * BANK_SLABS + s) * WORDS + u * P
+                        nc.tensor.transpose(bank[:, s, u, :], words[:, first : first + P], identity[:])
+                banks.append(bank)
+            return banks
+
+        def regroup_chunk(banks):
+            grouped = grouped_pool.tile([P, SLABS * P * PACK], BF16, align_bytes=64)
+            grouped_words = grouped[:].bitcast(F32).rearrange(
+                "p (s r u) -> p s r u", s=SLABS, u=HALVES
+            )
+            for b, bank in enumerate(banks):
+                nc.scalar.copy(
+                    out=grouped_words[:, b * BANK_SLABS : (b + 1) * BANK_SLABS],
+                    in_=bank[:].rearrange("p s u r -> p s r u"),
+                )
+            return grouped
+
+        def quantise_chunk(pool, grouped):
+            codes = pool.tile([P, SLABS * P], U32, align_bytes=64)
+            scales = pool.tile([P, SLABS * P], U8, align_bytes=64)
+            nc.vector.quantize_mx(out=codes[:].bitcast(FP8X4), scales=scales[:], in_=grouped[:])
+            return codes, scales
+
+        def mask_chunk(c):
+            for s in range(SLABS):
+                slab = m2_rows[c][:, s * K : (s + 1) * K]
+                neighbour = c * SLABS + s
+                nc.vector.tensor_scalar_mul(
+                    out=slab, in0=slab, scalar1=mask[:, neighbour : neighbour + 1]
+                )
+
+        acc = acc_pool.tile([P, CHANNELS], F32)
+
+        def multiply_chunk(c, codes, scales):
+            for s in range(SLABS):
+                neighbour = c * SLABS + s
+                nodes = slice(s * P, (s + 1) * P)
+                nc.tensor.matmul_mx(
+                    out=acc[:],
+                    lhsT=codes[:, nodes].bitcast(FP8X4),
+                    lhsT_scale=scales[:, nodes],
+                    rhs=w3_codes[:].bitcast(FP8X4),
+                    rhs_scale=w3_scales[:],
+                    start=(neighbour == 0),
+                    stop=(neighbour == NEIGHBOURS - 1),
+                )
+
+        w3_grouped = regroup_chunk(transpose_chunk(w3_rows))
+        mask_chunk(0)
+        w3_codes, w3_scales = quantise_chunk(keep, w3_grouped)
+
+        grouped_of = {}
+        mx_of = {}
+        for t in range(CHUNKS + 2):
+            if t < CHUNKS:
+                grouped_of[t] = regroup_chunk(transpose_chunk(m2_rows[t]))
+            if t + 1 < CHUNKS:
+                mask_chunk(t + 1)
+            if 1 <= t <= CHUNKS:
+                mx_of[t - 1] = quantise_chunk(mx_pool, grouped_of[t - 1])
+            if t >= 2:
+                multiply_chunk(t - 2, mx_of[t - 2][0], mx_of[t - 2][1])
+
+        kept = keep.tile([P, 1], F32)
+        nc.vector.tensor_reduce(out=kept[:], in_=mask[:], axis=mybir.AxisListType.X, op=ALU.add)
+        kept_scaled = keep.tile([P, 1], F32)
+        nc.vector.tensor_scalar_mul(out=kept_scaled[:], in0=kept[:], scalar1=1.0 / SCALE)
+        base = keep.tile([P, CHANNELS], F32)
+        nc.vector.scalar_tensor_tensor(
+            out=base[:], in0=b3_all[:], scalar=kept_scaled[:], in1=nodes_bf[:], op0=ALU.mult, op1=ALU.add
+        )
+
+        x = keep.tile([P, CHANNELS], F32)
+        nc.vector.scalar_tensor_tensor(
+            out=x[:], in0=acc[:], scalar=1.0 / SCALE, in1=base[:], op0=ALU.mult, op1=ALU.add
+        )
+        stats = keep.tile([P, 6], F32)
+        nc.vector.bn_stats(out=stats[:], in_=x[:])
+        mean_var = keep.tile([P, 2], F32)
+        nc.vector.bn_aggr(out=mean_var[:], in_=stats[:])
+        std = keep.tile([P, 1], F32)
+        nc.scalar.activation(out=std[:], in_=mean_var[:, 1:2], func=ACT.Sqrt, bias=eps[:], scale=1.0)
+        centred = keep.tile([P, CHANNELS], F32)
+        nc.vector.scalar_tensor_tensor(
+            out=centred[:], in0=x[:], scalar=mean_var[:, 0:1], in1=gain_all[:],
+            op0=ALU.subtract, op1=ALU.mult,
+        )
+        inv_std = keep.tile([P, 1], F32)
+        nc.vector.reciprocal(out=inv_std[:], in_=std[:])
+        result = keep.tile([P, CHANNELS], F32)
+        nc.vector.scalar_tensor_tensor(
+            out=result[:], in0=centred[:], scalar=inv_std[:], in1=shift_all[:],
+            op0=ALU.mult, op1=ALU.add,
+        )
+        nc.sync.dma_start(out=out, in_=result[:])

@@ -18,9 +18,11 @@ CHANNELS = 512
 PACK = 4
 WORDS = K // 2
 HALVES = WORDS // P
-SLABS = 4
-CHUNKS = NEIGHBOURS // SLABS
-BANK_SLABS = 2
+UNIT_SLABS = 2
+UNITS = NEIGHBOURS // UNIT_SLABS
+W3_UNITS = CHANNELS // (P * UNIT_SLABS)
+RUN = 4
+LAG = 2
 SCALE = 30.0
 EPS = 1e-5
 
@@ -34,24 +36,29 @@ def tile_decoderlayer_pb_kernel(
     with ExitStack() as ctx:
         ctx.enter_context(tc.manual_schedule())
         keep = ctx.enter_context(tc.tile_pool(name="keep", bufs=1))
-        grouped_pool = ctx.enter_context(tc.tile_pool(name="grouped", bufs=3))
-        mx_pool = ctx.enter_context(tc.tile_pool(name="mx", bufs=3))
-        bank_pool = ctx.enter_context(tc.psum_pool(name="banks", bufs=6))
+        grouped_pool = ctx.enter_context(tc.tile_pool(name="grouped", bufs=4))
+        mx_pool = ctx.enter_context(tc.tile_pool(name="mx", bufs=UNITS))
+        bank_pool = ctx.enter_context(tc.psum_pool(name="banks", bufs=7))
         acc_pool = ctx.enter_context(tc.psum_pool(name="acc", bufs=1))
 
         mask_bf = keep.tile([P, NEIGHBOURS], BF16)
         nc.sync.dma_start(out=mask_bf[:], in_=attention_mask)
-        w3_rows = keep.tile([P, SLABS * K], BF16)
-        nc.sync.dma_start(
-            out=w3_rows[:].rearrange("p (r k) -> p r k", r=SLABS),
-            in_=W3.rearrange("(r p) k -> p r k", p=P),
-        )
-        m2_rows = []
-        for c in range(CHUNKS):
-            rows = keep.tile([P, SLABS * K], BF16, name="m2_rows%d" % c)
+        w3_rows = []
+        for w in range(W3_UNITS):
+            rows = keep.tile([P, UNIT_SLABS * K], BF16, name="w3_rows%d" % w)
             nc.sync.dma_start(
-                out=rows[:].rearrange("p (s k) -> p s k", s=SLABS),
-                in_=m2[:, c * SLABS : (c + 1) * SLABS, :],
+                out=rows[:].rearrange("p (s k) -> p s k", s=UNIT_SLABS),
+                in_=W3[w * UNIT_SLABS * P : (w + 1) * UNIT_SLABS * P, :].rearrange(
+                    "(s p) k -> p s k", p=P
+                ),
+            )
+            w3_rows.append(rows)
+        m2_rows = []
+        for i in range(UNITS):
+            rows = keep.tile([P, UNIT_SLABS * K], BF16, name="m2_rows%d" % i)
+            nc.sync.dma_start(
+                out=rows[:].rearrange("p (s k) -> p s k", s=UNIT_SLABS),
+                in_=m2[:, i * UNIT_SLABS : (i + 1) * UNIT_SLABS, :],
             )
             m2_rows.append(rows)
         nodes_bf = keep.tile([P, CHANNELS], BF16)
@@ -71,76 +78,74 @@ def tile_decoderlayer_pb_kernel(
         nc.scalar.sqrt(out=table_warm[:], in_=eps[:])
         mask = keep.tile([P, NEIGHBOURS], F32)
         nc.vector.tensor_copy(out=mask[:], in_=mask_bf[:])
-
-        def transpose_chunk(rows):
-            words = rows[:].bitcast(F32)
-            banks = []
-            for b in range(SLABS // BANK_SLABS):
-                bank = bank_pool.tile([P, BANK_SLABS, HALVES, P], F32)
-                for s in range(BANK_SLABS):
-                    for u in range(HALVES):
-                        first = (b * BANK_SLABS + s) * WORDS + u * P
-                        nc.tensor.transpose(bank[:, s, u, :], words[:, first : first + P], identity[:])
-                banks.append(bank)
-            return banks
-
-        def regroup_chunk(banks):
-            grouped = grouped_pool.tile([P, SLABS * P * PACK], BF16, align_bytes=64)
-            grouped_words = grouped[:].bitcast(F32).rearrange(
-                "p (s r u) -> p s r u", s=SLABS, u=HALVES
+        kept_nodes = keep.tile([P, NEIGHBOURS, P], F32)
+        for k in range(NEIGHBOURS):
+            nc.vector.tensor_scalar_mul(
+                out=kept_nodes[:, k, :], in0=identity[:], scalar1=mask[:, k : k + 1]
             )
-            for b, bank in enumerate(banks):
-                nc.scalar.copy(
-                    out=grouped_words[:, b * BANK_SLABS : (b + 1) * BANK_SLABS],
-                    in_=bank[:].rearrange("p s u r -> p s r u"),
-                )
+
+        def transpose_unit(rows, selections):
+            words = rows[:].bitcast(F32)
+            bank = bank_pool.tile([P, UNIT_SLABS, HALVES, P], F32)
+            for s in range(UNIT_SLABS):
+                for u in range(HALVES):
+                    block = slice(s * WORDS + u * P, s * WORDS + (u + 1) * P)
+                    nc.tensor.transpose(bank[:, s, u, :], words[:, block], selections[s])
+            return bank
+
+        def regroup_unit(bank):
+            grouped = grouped_pool.tile([P, UNIT_SLABS * P * PACK], BF16, align_bytes=64)
+            nc.scalar.copy(
+                out=grouped[:].bitcast(F32).rearrange("p (s r u) -> p s r u", s=UNIT_SLABS, u=HALVES),
+                in_=bank[:].rearrange("p s u r -> p s r u"),
+            )
             return grouped
 
-        def quantise_chunk(pool, grouped):
-            codes = pool.tile([P, SLABS * P], U32, align_bytes=64)
-            scales = pool.tile([P, SLABS * P], U8, align_bytes=64)
-            nc.vector.quantize_mx(out=codes[:].bitcast(FP8X4), scales=scales[:], in_=grouped[:])
-            return codes, scales
+        def quantise_unit(grouped, codes, scales):
+            nc.vector.quantize_mx(out=codes.bitcast(FP8X4), scales=scales, in_=grouped[:])
 
-        def mask_chunk(c):
-            for s in range(SLABS):
-                slab = m2_rows[c][:, s * K : (s + 1) * K]
-                neighbour = c * SLABS + s
-                nc.vector.tensor_scalar_mul(
-                    out=slab, in0=slab, scalar1=mask[:, neighbour : neighbour + 1]
-                )
+        w3_codes = keep.tile([P, CHANNELS], U32, align_bytes=64)
+        w3_scales = keep.tile([P, CHANNELS], U8, align_bytes=64)
+        for w in range(W3_UNITS):
+            channels = slice(w * UNIT_SLABS * P, (w + 1) * UNIT_SLABS * P)
+            bank = transpose_unit(w3_rows[w], [identity[:]] * UNIT_SLABS)
+            quantise_unit(regroup_unit(bank), w3_codes[:, channels], w3_scales[:, channels])
 
         acc = acc_pool.tile([P, CHANNELS], F32)
+        m2_codes = {}
+        m2_scales = {}
 
-        def multiply_chunk(c, codes, scales):
-            for s in range(SLABS):
-                neighbour = c * SLABS + s
+        def prepare_unit(i):
+            selections = [kept_nodes[:, i * UNIT_SLABS + s, :] for s in range(UNIT_SLABS)]
+            bank = transpose_unit(m2_rows[i], selections)
+            codes = mx_pool.tile([P, UNIT_SLABS * P], U32, align_bytes=64)
+            scales = mx_pool.tile([P, UNIT_SLABS * P], U8, align_bytes=64)
+            quantise_unit(regroup_unit(bank), codes[:], scales[:])
+            m2_codes[i] = codes
+            m2_scales[i] = scales
+
+        def multiply_unit(i):
+            for s in range(UNIT_SLABS):
+                neighbour = i * UNIT_SLABS + s
                 nodes = slice(s * P, (s + 1) * P)
                 nc.tensor.matmul_mx(
                     out=acc[:],
-                    lhsT=codes[:, nodes].bitcast(FP8X4),
-                    lhsT_scale=scales[:, nodes],
+                    lhsT=m2_codes[i][:, nodes].bitcast(FP8X4),
+                    lhsT_scale=m2_scales[i][:, nodes],
                     rhs=w3_codes[:].bitcast(FP8X4),
                     rhs_scale=w3_scales[:],
                     start=(neighbour == 0),
                     stop=(neighbour == NEIGHBOURS - 1),
                 )
 
-        w3_grouped = regroup_chunk(transpose_chunk(w3_rows))
-        mask_chunk(0)
-        w3_codes, w3_scales = quantise_chunk(keep, w3_grouped)
-
-        grouped_of = {}
-        mx_of = {}
-        for t in range(CHUNKS + 2):
-            if t < CHUNKS:
-                grouped_of[t] = regroup_chunk(transpose_chunk(m2_rows[t]))
-            if t + 1 < CHUNKS:
-                mask_chunk(t + 1)
-            if 1 <= t <= CHUNKS:
-                mx_of[t - 1] = quantise_chunk(mx_pool, grouped_of[t - 1])
-            if t >= 2:
-                multiply_chunk(t - 2, mx_of[t - 2][0], mx_of[t - 2][1])
+        multiplied = 0
+        for first in range(0, UNITS, RUN):
+            for i in range(first, first + RUN):
+                prepare_unit(i)
+            ready = UNITS if first + RUN == UNITS else first + RUN - LAG
+            for i in range(multiplied, ready):
+                multiply_unit(i)
+            multiplied = ready
 
         kept = keep.tile([P, 1], F32)
         nc.vector.tensor_reduce(out=kept[:], in_=mask[:], axis=mybir.AxisListType.X, op=ALU.add)

@@ -79,10 +79,15 @@ def tile_decoderlayer_pb_kernel(
         mask = keep.tile([P, NEIGHBOURS], F32)
         nc.vector.tensor_copy(out=mask[:], in_=mask_bf[:])
         kept_nodes = keep.tile([P, NEIGHBOURS, P], F32)
-        for k in range(NEIGHBOURS):
-            nc.vector.tensor_scalar_mul(
-                out=kept_nodes[:, k, :], in0=identity[:], scalar1=mask[:, k : k + 1]
-            )
+
+        def select_unit(i):
+            for k in range(i * UNIT_SLABS, (i + 1) * UNIT_SLABS):
+                nc.vector.tensor_scalar_mul(
+                    out=kept_nodes[:, k, :], in0=identity[:], scalar1=mask[:, k : k + 1]
+                )
+
+        for i in range(RUN):
+            select_unit(i)
 
         def transpose_unit(rows, selections):
             words = rows[:].bitcast(F32)
@@ -116,6 +121,8 @@ def tile_decoderlayer_pb_kernel(
         m2_scales = {}
 
         def prepare_unit(i):
+            if i + RUN < UNITS:
+                select_unit(i + RUN)
             selections = [kept_nodes[:, i * UNIT_SLABS + s, :] for s in range(UNIT_SLABS)]
             bank = transpose_unit(m2_rows[i], selections)
             codes = mx_pool.tile([P, UNIT_SLABS * P], U32, align_bytes=64)

@@ -21,7 +21,7 @@ HALVES = WORDS // P
 UNIT_SLABS = 2
 UNITS = NEIGHBOURS // UNIT_SLABS
 W3_UNITS = CHANNELS // (P * UNIT_SLABS)
-RUN = 4
+RUN = 2
 LAG = 2
 SCALE = 30.0
 EPS = 1e-5
@@ -38,8 +38,8 @@ def tile_decoderlayer_pb_kernel(
         keep = ctx.enter_context(tc.tile_pool(name="keep", bufs=1))
         grouped_pool = ctx.enter_context(tc.tile_pool(name="grouped", bufs=4))
         mx_pool = ctx.enter_context(tc.tile_pool(name="mx", bufs=UNITS))
-        bank_pool = ctx.enter_context(tc.psum_pool(name="banks", bufs=7))
-        acc_pool = ctx.enter_context(tc.psum_pool(name="acc", bufs=1))
+        bank_pool = ctx.enter_context(tc.psum_pool(name="banks", bufs=4))
+        product_pool = ctx.enter_context(tc.psum_pool(name="products", bufs=4))
 
         mask_bf = keep.tile([P, NEIGHBOURS], BF16)
         nc.sync.dma_start(out=mask_bf[:], in_=attention_mask)
@@ -78,24 +78,14 @@ def tile_decoderlayer_pb_kernel(
         nc.scalar.sqrt(out=table_warm[:], in_=eps[:])
         mask = keep.tile([P, NEIGHBOURS], F32)
         nc.vector.tensor_copy(out=mask[:], in_=mask_bf[:])
-        kept_nodes = keep.tile([P, NEIGHBOURS, P], F32)
 
-        def select_unit(i):
-            for k in range(i * UNIT_SLABS, (i + 1) * UNIT_SLABS):
-                nc.vector.tensor_scalar_mul(
-                    out=kept_nodes[:, k, :], in0=identity[:], scalar1=mask[:, k : k + 1]
-                )
-
-        for i in range(RUN):
-            select_unit(i)
-
-        def transpose_unit(rows, selections):
+        def transpose_unit(rows):
             words = rows[:].bitcast(F32)
             bank = bank_pool.tile([P, UNIT_SLABS, HALVES, P], F32)
             for s in range(UNIT_SLABS):
                 for u in range(HALVES):
                     block = slice(s * WORDS + u * P, s * WORDS + (u + 1) * P)
-                    nc.tensor.transpose(bank[:, s, u, :], words[:, block], selections[s])
+                    nc.tensor.transpose(bank[:, s, u, :], words[:, block], identity[:])
             return bank
 
         def regroup_unit(bank):
@@ -113,18 +103,15 @@ def tile_decoderlayer_pb_kernel(
         w3_scales = keep.tile([P, CHANNELS], U8, align_bytes=64)
         for w in range(W3_UNITS):
             channels = slice(w * UNIT_SLABS * P, (w + 1) * UNIT_SLABS * P)
-            bank = transpose_unit(w3_rows[w], [identity[:]] * UNIT_SLABS)
+            bank = transpose_unit(w3_rows[w])
             quantise_unit(regroup_unit(bank), w3_codes[:, channels], w3_scales[:, channels])
 
-        acc = acc_pool.tile([P, CHANNELS], F32)
+        sums = [keep.tile([P, CHANNELS], F32, name="sum%d" % s) for s in range(UNIT_SLABS)]
         m2_codes = {}
         m2_scales = {}
 
         def prepare_unit(i):
-            if i + RUN < UNITS:
-                select_unit(i + RUN)
-            selections = [kept_nodes[:, i * UNIT_SLABS + s, :] for s in range(UNIT_SLABS)]
-            bank = transpose_unit(m2_rows[i], selections)
+            bank = transpose_unit(m2_rows[i])
             codes = mx_pool.tile([P, UNIT_SLABS * P], U32, align_bytes=64)
             scales = mx_pool.tile([P, UNIT_SLABS * P], U8, align_bytes=64)
             quantise_unit(regroup_unit(bank), codes[:], scales[:])
@@ -135,15 +122,24 @@ def tile_decoderlayer_pb_kernel(
             for s in range(UNIT_SLABS):
                 neighbour = i * UNIT_SLABS + s
                 nodes = slice(s * P, (s + 1) * P)
+                product = product_pool.tile([P, CHANNELS], F32)
                 nc.tensor.matmul_mx(
-                    out=acc[:],
+                    out=product[:],
                     lhsT=m2_codes[i][:, nodes].bitcast(FP8X4),
                     lhsT_scale=m2_scales[i][:, nodes],
                     rhs=w3_codes[:].bitcast(FP8X4),
                     rhs_scale=w3_scales[:],
-                    start=(neighbour == 0),
-                    stop=(neighbour == NEIGHBOURS - 1),
+                    start=True,
+                    stop=True,
                 )
+                kept_column = mask[:, neighbour : neighbour + 1]
+                if i == 0:
+                    nc.vector.tensor_scalar_mul(out=sums[s][:], in0=product[:], scalar1=kept_column)
+                else:
+                    nc.vector.scalar_tensor_tensor(
+                        out=sums[s][:], in0=product[:], scalar=kept_column, in1=sums[s][:],
+                        op0=ALU.mult, op1=ALU.add,
+                    )
 
         multiplied = 0
         for first in range(0, UNITS, RUN):
@@ -163,9 +159,11 @@ def tile_decoderlayer_pb_kernel(
             out=base[:], in0=b3_all[:], scalar=kept_scaled[:], in1=nodes_bf[:], op0=ALU.mult, op1=ALU.add
         )
 
+        total = keep.tile([P, CHANNELS], F32)
+        nc.vector.tensor_add(out=total[:], in0=sums[0][:], in1=sums[1][:])
         x = keep.tile([P, CHANNELS], F32)
         nc.vector.scalar_tensor_tensor(
-            out=x[:], in0=acc[:], scalar=1.0 / SCALE, in1=base[:], op0=ALU.mult, op1=ALU.add
+            out=x[:], in0=total[:], scalar=1.0 / SCALE, in1=base[:], op0=ALU.mult, op1=ALU.add
         )
         stats = keep.tile([P, 6], F32)
         nc.vector.bn_stats(out=stats[:], in_=x[:])

from contextlib import ExitStack

import concourse.mybir as mybir
from concourse.masks import make_identity

F32 = mybir.dt.float32
BF16 = mybir.dt.bfloat16
U32 = mybir.dt.uint32
U8 = mybir.dt.uint8
FP8X4 = mybir.dt.float8_e4m3fn_x4
ALU = mybir.AluOpType
ACT = mybir.ActivationFunctionType

P = 128
NEIGHBOURS = 32
K = 512
CHANNELS = 512
PACK = 4
WORDS = K // 2
HALVES = WORDS // P
UNIT_SLABS = 2
UNITS = NEIGHBOURS // UNIT_SLABS
W3_UNITS = CHANNELS // (P * UNIT_SLABS)
RUN = 2
LAG = 2
SCALE = 30.0
EPS = 1e-5

FLOPS = 2 * P * NEIGHBOURS * K * CHANNELS


def tile_decoderlayer_pb_kernel(
    tc, m2, W3, b3, attention_mask, node_features, ln1_w, ln1_b, out
):
    nc = tc.nc
    with ExitStack() as ctx:
        ctx.enter_context(tc.manual_schedule())
        keep = ctx.enter_context(tc.tile_pool(name="keep", bufs=1))
        grouped_pool = ctx.enter_context(tc.tile_pool(name="grouped", bufs=4))
        mx_pool = ctx.enter_context(tc.tile_pool(name="mx", bufs=UNITS))
        bank_pool = ctx.enter_context(tc.psum_pool(name="banks", bufs=4))
        product_pool = ctx.enter_context(tc.psum_pool(name="products", bufs=4))

        mask_bf = keep.tile([P, NEIGHBOURS], BF16)
        nc.sync.dma_start(out=mask_bf[:], in_=attention_mask)
        w3_rows = []
        for w in range(W3_UNITS):
            rows = keep.tile([P, UNIT_SLABS * K], BF16, name="w3_rows%d" % w)
            nc.sync.dma_start(
                out=rows[:].rearrange("p (s k) -> p s k", s=UNIT_SLABS),
                in_=W3[w * UNIT_SLABS * P : (w + 1) * UNIT_SLABS * P, :].rearrange(
                    "(s p) k -> p s k", p=P
                ),
            )
            w3_rows.append(rows)
        m2_rows = []
        for i in range(UNITS):
            rows = keep.tile([P, UNIT_SLABS * K], BF16, name="m2_rows%d" % i)
            nc.sync.dma_start(
                out=rows[:].rearrange("p (s k) -> p s k", s=UNIT_SLABS),
                in_=m2[:, i * UNIT_SLABS : (i + 1) * UNIT_SLABS, :],
            )
            m2_rows.append(rows)
        nodes_bf = keep.tile([P, CHANNELS], BF16)
        nc.sync.dma_start(out=nodes_bf[:], in_=node_features)
        b3_all = keep.tile([P, CHANNELS], BF16)
        nc.sync.dma_start(out=b3_all[:], in_=b3.partition_broadcast(P))
        gain_all = keep.tile([P, CHANNELS], BF16)
        nc.sync.dma_start(out=gain_all[:], in_=ln1_w.partition_broadcast(P))
        shift_all = keep.tile([P, CHANNELS], BF16)
        nc.sync.dma_start(out=shift_all[:], in_=ln1_b.partition_broadcast(P))

        identity = keep.tile([P, P], F32)
        make_identity(nc, identity[:])
        eps = keep.tile([P, 1], F32)
        nc.vector.memset(eps[:], EPS)
        table_warm = keep.tile([P, 1], F32)
        nc.scalar.sqrt(out=table_warm[:], in_=eps[:])
        mask = keep.tile([P, NEIGHBOURS], F32)
        nc.vector.tensor_copy(out=mask[:], in_=mask_bf[:])

        def transpose_unit(rows):
            words = rows[:].bitcast(F32)
            bank = bank_pool.tile([P, UNIT_SLABS, HALVES, P], F32)
            for s in range(UNIT_SLABS):
                for u in range(HALVES):
                    block = slice(s * WORDS + u * P, s * WORDS + (u + 1) * P)
                    nc.tensor.transpose(bank[:, s, u, :], words[:, block], identity[:])
            return bank

        def regroup_unit(bank):
            grouped = grouped_pool.tile([P, UNIT_SLABS * P * PACK], BF16, align_bytes=64)
            nc.scalar.copy(
                out=grouped[:].bitcast(F32).rearrange("p (s r u) -> p s r u", s=UNIT_SLABS, u=HALVES),
                in_=bank[:].rearrange("p s u r -> p s r u"),
            )
            return grouped

        def quantise_unit(grouped, codes, scales):
            nc.vector.quantize_mx(out=codes.bitcast(FP8X4), scales=scales, in_=grouped[:])

        w3_codes = keep.tile([P, CHANNELS], U32, align_bytes=64)
        w3_scales = keep.tile([P, CHANNELS], U8, align_bytes=64)
        for w in range(W3_UNITS):
            channels = slice(w * UNIT_SLABS * P, (w + 1) * UNIT_SLABS * P)
            bank = transpose_unit(w3_rows[w])
            quantise_unit(regroup_unit(bank), w3_codes[:, channels], w3_scales[:, channels])

        sums = [keep.tile([P, CHANNELS], F32, name="sum%d" % s) for s in range(UNIT_SLABS)]
        m2_codes = {}
        m2_scales = {}

        def prepare_unit(i):
            bank = transpose_unit(m2_rows[i])
            codes = mx_pool.tile([P, UNIT_SLABS * P], U32, align_bytes=64)
            scales = mx_pool.tile([P, UNIT_SLABS * P], U8, align_bytes=64)
            quantise_unit(regroup_unit(bank), codes[:], scales[:])
            m2_codes[i] = codes
            m2_scales[i] = scales

        def multiply_unit(i):
            for s in range(UNIT_SLABS):
                neighbour = i * UNIT_SLABS + s
                nodes = slice(s * P, (s + 1) * P)
                product = product_pool.tile([P, CHANNELS], F32)
                nc.tensor.matmul_mx(
                    out=product[:],
                    lhsT=m2_codes[i][:, nodes].bitcast(FP8X4),
                    lhsT_scale=m2_scales[i][:, nodes],
                    rhs=w3_codes[:].bitcast(FP8X4),
                    rhs_scale=w3_scales[:],
                    start=True,
                    stop=True,
                )
                kept_column = mask[:, neighbour : neighbour + 1]
                if i == 0:
                    nc.vector.tensor_scalar_mul(out=sums[s][:], in0=product[:], scalar1=kept_column)
                else:
                    nc.vector.scalar_tensor_tensor(
                        out=sums[s][:], in0=product[:], scalar=kept_column, in1=sums[s][:],
                        op0=ALU.mult, op1=ALU.add,
                    )

        multiplied = 0
        for first in range(0, UNITS, RUN):
            for i in range(first, first + RUN):
                prepare_unit(i)
            ready = UNITS if first + RUN == UNITS else first + RUN - LAG
            for i in range(multiplied, ready):
                multiply_unit(i)
            multiplied = ready

        kept = keep.tile([P, 1], F32)
        nc.vector.tensor_reduce(out=kept[:], in_=mask[:], axis=mybir.AxisListType.X, op=ALU.add)
        kept_scaled = keep.tile([P, 1], F32)
        nc.vector.tensor_scalar_mul(out=kept_scaled[:], in0=kept[:], scalar1=1.0 / SCALE)
        base = keep.tile([P, CHANNELS], F32)
        nc.vector.scalar_tensor_tensor(
            out=base[:], in0=b3_all[:], scalar=kept_scaled[:], in1=nodes_bf[:], op0=ALU.mult, op1=ALU.add
        )

        total = keep.tile([P, CHANNELS], F32)
        nc.vector.tensor_add(out=total[:], in0=sums[0][:], in1=sums[1][:])
        x = keep.tile([P, CHANNELS], F32)
        nc.vector.scalar_tensor_tensor(
            out=x[:], in0=total[:], scalar=1.0 / SCALE, in1=base[:], op0=ALU.mult, op1=ALU.add
        )
        stats = keep.tile([P, 6], F32)
        nc.vector.bn_stats(out=stats[:], in_=x[:])
        mean_var = keep.tile([P, 2], F32)
        nc.vector.bn_aggr(out=mean_var[:], in_=stats[:])
        std = keep.tile([P, 1], F32)
        nc.scalar.activation(out=std[:], in_=mean_var[:, 1:2], func=ACT.Sqrt, bias=eps[:], scale=1.0)
        centred = keep.tile([P, CHANNELS], F32)
        nc.vector.scalar_tensor_tensor(
            out=centred[:], in0=x[:], scalar=mean_var[:, 0:1], in1=gain_all[:],
            op0=ALU.subtract, op1=ALU.mult,
        )
        inv_std = keep.tile([P, 1], F32)
        nc.vector.reciprocal(out=inv_std[:], in_=std[:])
        result = keep.tile([P, CHANNELS], F32)
        nc.vector.scalar_tensor_tensor(
            out=result[:], in0=centred[:], scalar=inv_std[:], in1=shift_all[:],
            op0=ALU.mult, op1=ALU.add,
        )
        nc.sync.dma_start(out=out, in_=result[:])
